import numpy as np
import ml_dtypes


def mxq(x, axis, fmt="e4m3"):
    dtype, down = {"e4m3": (ml_dtypes.float8_e4m3fn, 7), "e5m2": (ml_dtypes.float8_e5m2, 14)}[fmt]
    v = np.moveaxis(np.asarray(x, np.float32).astype(ml_dtypes.bfloat16).astype(np.float64), axis, -1)
    blocks = v.reshape(v.shape[:-1] + (-1, 32))
    amax = np.abs(blocks).max(-1, keepdims=True)
    byte = np.maximum(np.where(amax > 0, np.frexp(amax)[1] - 1 + 127, 0) - down, 1)
    scale = np.exp2(byte - 127.0)
    codes = (blocks / scale).astype(np.float32).astype(dtype).astype(np.float64)
    return np.moveaxis((codes * scale).reshape(v.shape), -1, axis)


WIDE = False


def mx_kscale(k):
    if not WIDE:
        return np.ones(k)
    levels = np.array([10, -10, 5, -5, 0])
    if k % 512:
        return np.exp2(np.random.permutation(np.resize(levels, k // 32))).repeat(32)
    a = np.empty((k // 512, 16))
    for p in range(k // 512):
        a[p, :8] = np.random.permutation(np.resize(levels, 8))
        for g in range(8):
            far = levels[np.abs(levels - a[p, g]) >= 10]
            a[p, g + 8] = far[np.random.randint(len(far))]
    return np.exp2(a.ravel()).repeat(32)


BF16 = ml_dtypes.bfloat16


def bf(x):
    return np.asarray(x, np.float32).astype(BF16)


def f64(x):
    return np.asarray(x).astype(np.float64)


B, K, N = 8192, 512, 256
EPS = 1e-5
GELU_C = 0.7978845608


def setup_inputs():
    s = mx_kscale(K)
    return {"x": bf(np.random.standard_normal((B, K)) * s),
            "weight": bf(np.random.standard_normal((K, N)) * np.sqrt(2.0 / K) / s[:, None]),
            "bn_gamma": bf(np.random.uniform(0.5, 1.5, N)),
            "bn_beta": bf(np.random.standard_normal(N) * 0.1),
            "bn_mean": bf(np.random.standard_normal(N) * 0.1),
            "bn_var": bf(np.random.uniform(0.5, 1.5, N))}


def reference(x, weight, bn_gamma, bn_beta, bn_mean, bn_var):
    acc = mxq(f64(x), 1, "e4m3") @ mxq(f64(weight), 0, "e4m3")
    x_norm = (acc - f64(bn_mean)) / np.sqrt(f64(bn_var) + EPS)
    bn_out = f64(bn_gamma) * x_norm + f64(bn_beta)
    gelu = 0.5 * bn_out * (1.0 + np.tanh(GELU_C * (bn_out + 0.044715 * bn_out * bn_out * bn_out)))
    return np.maximum(gelu, 0.0)

@@ -1,0 +1,249 @@
+from contextlib import ExitStack
+
+import concourse.masks as masks
+import concourse.mybir as mybir
+
+F32 = mybir.dt.float32
+BF16 = mybir.dt.bfloat16
+U32 = mybir.dt.uint32
+U8 = mybir.dt.uint8
+FP8X4 = mybir.dt.float8_e4m3fn_x4
+ACT = mybir.ActivationFunctionType
+ALU = mybir.AluOpType
+
+P = 128
+B, K, N = 8192, 512, 256
+EPS = 1e-5
+FLOPS = 2 * B * K * N
+
+UNIT = 512
+J = UNIT // P
+NU = B // UNIT
+LA = 2
+LG = 2
+
+
+def tile_modelnew_t_kernel(tc, x, weight, bn_gamma, bn_beta, bn_mean, bn_var, out):
+    nc = tc.nc
+    with ExitStack() as ctx:
+        const = ctx.enter_context(tc.tile_pool(name="const", bufs=1))
+        xin = ctx.enter_context(tc.tile_pool(name="xin", bufs=1))
+        work = ctx.enter_context(tc.tile_pool(name="work", bufs=3))
+        gpool = ctx.enter_context(tc.tile_pool(name="gpool", bufs=6))
+        opool = ctx.enter_context(tc.tile_pool(name="opool", bufs=1))
+        psum = ctx.enter_context(tc.psum_pool(name="psum", bufs=1))
+
+        prm_rows = const.tile([8, P], BF16)
+        for v, vec in enumerate((bn_gamma, bn_beta, bn_mean, bn_var)):
+            nc.scalar.dma_start(
+                out=prm_rows[2 * v : 2 * v + 2, :], in_=vec.rearrange("(h n) -> h n", h=2)
+            )
+        x_words = {}
+        w_raw = const.tile([P, 4, N], BF16)
+        for c in range(NU):
+            rows = x[c * UNIT : (c + 1) * UNIT, :].rearrange("(p j) k -> p j k", j=J)
+            if c == 0:
+                for hb in range(2):
+                    half = xin.tile([P, 2, K], BF16, name="x0_%d" % hb)
+                    nc.sync.dma_start(out=half[:], in_=rows[:, 2 * hb : 2 * hb + 2, :])
+                    x_words[(c, hb)] = half[:].rearrange("p j k -> p (j k)").bitcast(F32)
+                nc.sync.dma_start(
+                    out=w_raw[:], in_=weight.rearrange("(p t) n -> p t n", t=4)
+                )
+            else:
+                whole = xin.tile([P, J, K], BF16, name="x%d" % c)
+                nc.sync.dma_start(out=whole[:], in_=rows)
+                for hb in range(2):
+                    x_words[(c, hb)] = (
+                        whole[:, 2 * hb : 2 * hb + 2, :].rearrange("p j k -> p (j k)").bitcast(F32)
+                    )
+
+        warm = const.tile([P, 1], F32)
+        nc.vector.memset(warm[:], 0.0)
+        warm2 = const.tile([P, 1], F32)
+        nc.scalar.activation(out=warm2[:], in_=warm[:], func=ACT.Gelu_apprx_tanh)
+        ident = const.tile([P, P], F32)
+        masks.make_identity(nc, ident[:])
+        prm_f = const.tile([P, P], F32)
+        nc.vector.memset(prm_f[:], 0.0)
+        mhalf = const.tile([P, 2], F32)
+        nc.vector.memset(mhalf[:], -0.5)
+
+        w_grp = const.tile([P, N, 4], BF16, align_bytes=64)
+        w_codes = const.tile([P, N], U32, align_bytes=64)
+        w_scales = const.tile([P, N], U8, align_bytes=64)
+        bn_s = const.tile([P, 2], F32)
+        bn_b = const.tile([P, 2], F32)
+
+        def prep_weight():
+            nc.vector.tensor_copy(
+                out=w_grp[:], in_=w_raw[:].rearrange("p t n -> p n t")
+            )
+            nc.vector.quantize_mx(
+                out=w_codes[:].bitcast(FP8X4),
+                scales=w_scales[:],
+                in_=w_grp[:].rearrange("p n t -> p (n t)"),
+            )
+
+        p_t = psum.tile([P, P], F32, tag="ot", bufs=2)
+        prm = const.tile([P, 8], F32)
+        veps = const.tile([P, 2], F32)
+        rstd = const.tile([P, 2], F32)
+        ms = const.tile([P, 2], F32)
+
+        def prep_bn_1():
+            nc.vector.tensor_copy(out=prm_f[0:8, :], in_=prm_rows[:])
+            nc.tensor.transpose(p_t[:], prm_f[:], ident[:])
+
+        def prep_bn_2():
+            nc.vector.tensor_copy(out=prm[:], in_=p_t[:, 0:8])
+            nc.vector.tensor_scalar_add(out=veps[:], in0=prm[:, 6:8], scalar1=EPS)
+            nc.gpsimd.tensor_tensor(out=rstd[:], in0=veps[:], in1=mhalf[:], op=ALU.pow)
+
+        def prep_bn_3():
+            nc.vector.tensor_mul(out=bn_s[:], in0=prm[:, 0:2], in1=rstd[:])
+            nc.vector.tensor_mul(out=ms[:], in0=prm[:, 4:6], in1=bn_s[:])
+            nc.vector.tensor_sub(out=bn_b[:], in0=prm[:, 2:4], in1=ms[:])
+
+        xt = {}
+        grp = {}
+        xq = {}
+        acc = {}
+        gel = {}
+        ot = {}
+        o_sb = {}
+
+        def stage_a(i):
+            for hb in range(2):
+                words = x_words[(i, hb)]
+                t = psum.tile([P, 2, 2, P], F32, tag="xt", bufs=3, name="xt%d_%d" % (i, hb))
+                for jj in range(2):
+                    for u in range(2):
+                        col = jj * (K // 2) + u
+                        nc.tensor.transpose(
+                            t[:, jj, u, :], words[:, col : (jj + 1) * (K // 2) : 2], ident[:]
+                        )
+                xt[(i, hb)] = t
+
+        def stage_b(i, hb, eng):
+            if hb == 0:
+                grp[i] = work.tile([P, 4 * UNIT], BF16, tag="grp", align_bytes=64, name="grp%d" % i)
+            dst = grp[i][:].bitcast(F32)[:, hb * UNIT : (hb + 1) * UNIT].rearrange(
+                "p (j r u) -> p j r u", j=2, u=2
+            )
+            src = xt[(i, hb)][:].rearrange("p j u r -> p j r u")
+            if eng == "V":
+                nc.vector.tensor_copy(out=dst, in_=src)
+            else:
+                nc.scalar.copy(out=dst, in_=src)
+
+        def stage_c(i):
+            codes = work.tile([P, UNIT], U32, tag="xq", align_bytes=64, name="xq%d" % i)
+            scales = work.tile([P, UNIT], U8, tag="xs", align_bytes=64, name="xs%d" % i)
+            nc.vector.quantize_mx(out=codes[:].bitcast(FP8X4), scales=scales[:], in_=grp[i][:])
+            xq[i] = (codes, scales)
+
+        def stage_d(i):
+            codes, scales = xq[i]
+            for h in range(2):
+                a = psum.tile([P, UNIT], F32, tag="acc", bufs=3, name="acc%d_%d" % (i, h))
+                nc.tensor.matmul_mx(
+                    out=a[:],
+                    lhsT=w_codes[:, h * P : (h + 1) * P].bitcast(FP8X4),
+                    lhsT_scale=w_scales[:, h * P : (h + 1) * P],
+                    rhs=codes[:].bitcast(FP8X4),
+                    rhs_scale=scales[:],
+                    start=True,
+                    stop=True,
+                )
+                acc[(i, h)] = a
+
+        def stage_e(i):
+            for h in range(2):
+                g = gpool.tile([P, UNIT], F32, tag="g", name="g%d_%d" % (i, h))
+                nc.scalar.activation(
+                    out=g[:],
+                    in_=acc[(i, h)][:],
+                    func=ACT.Gelu_apprx_tanh,
+                    bias=bn_b[:, h : h + 1],
+                    scale=bn_s[:, h : h + 1],
+                )
+                gel[(i, h)] = g
+
+        def stage_f(i):
+            for hb in range(2):
+                t = psum.tile([P, 2, N], F32, tag="ot", bufs=2, name="ot%d_%d" % (i, hb))
+                for jj in range(2):
+                    for h in range(2):
+                        col = (2 * hb + jj) * P
+                        nc.tensor.transpose(
+                            t[:, jj, h * P : (h + 1) * P], gel[(i, h)][:, col : col + P], ident[:]
+                        )
+                ot[(i, hb)] = t
+
+        def stage_g(i, hb, eng):
+            if i == NU - 1:
+                o_sb[(i, hb)] = opool.tile([P, 2 * N], F32, name="o%d_%d" % (i, hb))
+                dst = o_sb[(i, hb)][:]
+            else:
+                if hb == 0:
+                    o_sb[i] = opool.tile([P, J * N], F32, name="o%d" % i)
+                dst = o_sb[i][:, hb * 2 * N : (hb + 1) * 2 * N]
+            src = ot[(i, hb)][:].rearrange("p j n -> p (j n)")
+            if eng == "V":
+                nc.vector.tensor_scalar(
+                    out=dst, in0=src, scalar1=0.0, scalar2=0.0, op0=ALU.max, op1=ALU.add
+                )
+            else:
+                nc.scalar.activation(out=dst, in_=src, func=ACT.Relu)
+
+        def stage_h(i):
+            rows = out[i * UNIT : (i + 1) * UNIT, :].rearrange("(p j) n -> p j n", j=J)
+            if i == NU - 1:
+                for hb in range(2):
+                    nc.sync.dma_start(
+                        out=rows[:, 2 * hb : 2 * hb + 2, :],
+                        in_=o_sb[(i, hb)][:].rearrange("p (j n) -> p j n", j=2),
+                    )
+            else:
+                nc.sync.dma_start(out=rows, in_=o_sb[i][:].rearrange("p (j n) -> p j n", j=J))
+
+        def b_engine(i, hb):
+            return "S" if (i < 3 and hb == 1) else "V"
+
+        def g_engine(i, hb):
+            if i == NU - 1:
+                return "V" if hb == 0 else "S"
+            if i >= NU - 3:
+                return "V"
+            if hb == 1:
+                return "S"
+            return "V" if i % 4 == 0 else "S"
+
+        def live(i):
+            return 0 <= i < NU
+
+        for p in range(-LA, NU + LG + 1):
+            if live(p + 1):
+                stage_c(p + 1)
+            if live(p):
+                stage_d(p)
+            if live(p + LA):
+                stage_a(p + LA)
+            if live(p - 1):
+                stage_f(p - 1)
+            if live(p - LG):
+                stage_g(p - LG, 0, g_engine(p - LG, 0))
+                stage_g(p - LG, 1, g_engine(p - LG, 1))
+                stage_h(p - LG)
+            if live(p):
+                stage_e(p)
+            if live(p + LA):
+                stage_b(p + LA, 0, b_engine(p + LA, 0))
+                stage_b(p + LA, 1, b_engine(p + LA, 1))
+            if p == -LA:
+                prep_bn_1()
+                prep_weight()
+                prep_bn_2()
+            if p == -LA + 1:
+                prep_bn_3()

@@ -16,11 +16,10 @@ B, K, N = 8192, 512, 256
 EPS = 1e-5
 FLOPS = 2 * B * K * N
 
-UNIT = 512
-J = UNIT // P
-NU = B // UNIT
+HALF = 256
+CHUNKS = [256, 256] + [512] * 14 + [256, 256]
+NC = len(CHUNKS)
 LA = 2
-LG = 2
 
 
 def tile_modelnew_t_kernel(tc, x, weight, bn_gamma, bn_beta, bn_mean, bn_var, out):
@@ -28,35 +27,29 @@ def tile_modelnew_t_kernel(tc, x, weight, bn_gamma, bn_beta, bn_mean, bn_var, ou
     with ExitStack() as ctx:
         const = ctx.enter_context(tc.tile_pool(name="const", bufs=1))
         xin = ctx.enter_context(tc.tile_pool(name="xin", bufs=1))
-        work = ctx.enter_context(tc.tile_pool(name="work", bufs=3))
+        work = ctx.enter_context(tc.tile_pool(name="work", bufs=4))
         gpool = ctx.enter_context(tc.tile_pool(name="gpool", bufs=6))
         opool = ctx.enter_context(tc.tile_pool(name="opool", bufs=1))
         psum = ctx.enter_context(tc.psum_pool(name="psum", bufs=1))
+        ctx.enter_context(tc.manual_schedule())
 
         prm_rows = const.tile([8, P], BF16)
-        for v, vec in enumerate((bn_gamma, bn_beta, bn_mean, bn_var)):
-            nc.scalar.dma_start(
-                out=prm_rows[2 * v : 2 * v + 2, :], in_=vec.rearrange("(h n) -> h n", h=2)
-            )
-        x_words = {}
+        starts = [sum(CHUNKS[:i]) for i in range(NC)]
+        x_sb = {}
         w_raw = const.tile([P, 4, N], BF16)
-        for c in range(NU):
-            rows = x[c * UNIT : (c + 1) * UNIT, :].rearrange("(p j) k -> p j k", j=J)
-            if c == 0:
-                for hb in range(2):
-                    half = xin.tile([P, 2, K], BF16, name="x0_%d" % hb)
-                    nc.sync.dma_start(out=half[:], in_=rows[:, 2 * hb : 2 * hb + 2, :])
-                    x_words[(c, hb)] = half[:].rearrange("p j k -> p (j k)").bitcast(F32)
-                nc.sync.dma_start(
-                    out=w_raw[:], in_=weight.rearrange("(p t) n -> p t n", t=4)
-                )
-            else:
-                whole = xin.tile([P, J, K], BF16, name="x%d" % c)
-                nc.sync.dma_start(out=whole[:], in_=rows)
-                for hb in range(2):
-                    x_words[(c, hb)] = (
-                        whole[:, 2 * hb : 2 * hb + 2, :].rearrange("p j k -> p (j k)").bitcast(F32)
+        for i in range(NC):
+            rows = x[starts[i] : starts[i] + CHUNKS[i], :].rearrange(
+                "(p j) k -> p j k", j=CHUNKS[i] // P
+            )
+            t = xin.tile([P, CHUNKS[i] // P, K], BF16, name="x%d" % i)
+            nc.sync.dma_start(out=t[:], in_=rows)
+            x_sb[i] = t
+            if i == 0:
+                for v, vec in enumerate((bn_gamma, bn_beta, bn_mean, bn_var)):
+                    nc.sync.dma_start(
+                        out=prm_rows[2 * v : 2 * v + 2, :], in_=vec.rearrange("(h n) -> h n", h=2)
                     )
+                nc.sync.dma_start(out=w_raw[:], in_=weight.rearrange("(p t) n -> p t n", t=4))
 
         warm = const.tile([P, 1], F32)
         nc.vector.memset(warm[:], 0.0)
@@ -74,37 +67,13 @@ def tile_modelnew_t_kernel(tc, x, weight, bn_gamma, bn_beta, bn_mean, bn_var, ou
         w_scales = const.tile([P, N], U8, align_bytes=64)
         bn_s = const.tile([P, 2], F32)
         bn_b = const.tile([P, 2], F32)
-
-        def prep_weight():
-            nc.vector.tensor_copy(
-                out=w_grp[:], in_=w_raw[:].rearrange("p t n -> p n t")
-            )
-            nc.vector.quantize_mx(
-                out=w_codes[:].bitcast(FP8X4),
-                scales=w_scales[:],
-                in_=w_grp[:].rearrange("p n t -> p (n t)"),
-            )
-
-        p_t = psum.tile([P, P], F32, tag="ot", bufs=2)
+        p_t = psum.tile([P, P], F32, tag="ot", bufs=3)
         prm = const.tile([P, 8], F32)
         veps = const.tile([P, 2], F32)
         rstd = const.tile([P, 2], F32)
         ms = const.tile([P, 2], F32)
 
-        def prep_bn_1():
-            nc.vector.tensor_copy(out=prm_f[0:8, :], in_=prm_rows[:])
-            nc.tensor.transpose(p_t[:], prm_f[:], ident[:])
-
-        def prep_bn_2():
-            nc.vector.tensor_copy(out=prm[:], in_=p_t[:, 0:8])
-            nc.vector.tensor_scalar_add(out=veps[:], in0=prm[:, 6:8], scalar1=EPS)
-            nc.gpsimd.tensor_tensor(out=rstd[:], in0=veps[:], in1=mhalf[:], op=ALU.pow)
-
-        def prep_bn_3():
-            nc.vector.tensor_mul(out=bn_s[:], in0=prm[:, 0:2], in1=rstd[:])
-            nc.vector.tensor_mul(out=ms[:], in0=prm[:, 4:6], in1=bn_s[:])
-            nc.vector.tensor_sub(out=bn_b[:], in0=prm[:, 2:4], in1=ms[:])
-
+        split = {}
         xt = {}
         grp = {}
         xq = {}
@@ -113,137 +82,189 @@ def tile_modelnew_t_kernel(tc, x, weight, bn_gamma, bn_beta, bn_mean, bn_var, ou
         ot = {}
         o_sb = {}
 
-        def stage_a(i):
-            for hb in range(2):
-                words = x_words[(i, hb)]
-                t = psum.tile([P, 2, 2, P], F32, tag="xt", bufs=3, name="xt%d_%d" % (i, hb))
-                for jj in range(2):
-                    for u in range(2):
-                        col = jj * (K // 2) + u
-                        nc.tensor.transpose(
-                            t[:, jj, u, :], words[:, col : (jj + 1) * (K // 2) : 2], ident[:]
-                        )
-                xt[(i, hb)] = t
+        def halves(i):
+            return range(max(1, CHUNKS[i] // HALF))
 
-        def stage_b(i, hb, eng):
-            if hb == 0:
-                grp[i] = work.tile([P, 4 * UNIT], BF16, tag="grp", align_bytes=64, name="grp%d" % i)
-            dst = grp[i][:].bitcast(F32)[:, hb * UNIT : (hb + 1) * UNIT].rearrange(
-                "p (j r u) -> p j r u", j=2, u=2
+        def groups(i):
+            return min(2, CHUNKS[i] // P)
+
+        def words(i, h):
+            g = groups(i)
+            return x_sb[i][:, 2 * h : 2 * h + g, :].rearrange("p j k -> p (j k)").bitcast(F32)
+
+        def is_split(i, h):
+            return i >= 3 and (h == 1 or i % 2 == 0)
+
+        def out_engine(i, h):
+            return "V" if i >= NC - 4 or (h == 0 and i % 3 == 0) else "S"
+
+        def in_engine(i, h):
+            return "S" if i == 0 or (i <= LA + 2 and h == 1) else "V"
+
+        def stage_z(i, h):
+            g = groups(i)
+            t = work.tile([P, g, 2, P], F32, tag="z", name="z%d_%d" % (i, h))
+            nc.vector.tensor_copy(
+                out=t[:], in_=words(i, h).rearrange("p (j w u) -> p j u w", j=g, u=2)
             )
-            src = xt[(i, hb)][:].rearrange("p j u r -> p j r u")
-            if eng == "V":
+            split[(i, h)] = t
+
+        def stage_a(i, h):
+            g = groups(i)
+            t = psum.tile([P, g, 2, P], F32, tag="xt", bufs=3, name="xt%d_%d" % (i, h))
+            for jj in range(g):
+                for u in range(2):
+                    if is_split(i, h):
+                        src = split[(i, h)][:, jj, u, :]
+                    else:
+                        src = words(i, h)[:, jj * (K // 2) + u : (jj + 1) * (K // 2) : 2]
+                    nc.tensor.transpose(t[:, jj, u, :], src, ident[:])
+            xt[(i, h)] = t
+
+        def stage_b(i, h):
+            if i not in grp:
+                grp[i] = work.tile(
+                    [P, 4 * CHUNKS[i]], BF16, tag="grp", align_bytes=64, name="grp%d" % i
+                )
+            g = groups(i)
+            dst = (
+                grp[i][:]
+                .bitcast(F32)[:, h * 2 * HALF : h * 2 * HALF + g * 2 * P]
+                .rearrange("p (j r u) -> p j r u", j=g, u=2)
+            )
+            src = xt[(i, h)][:].rearrange("p j u r -> p j r u")
+            if in_engine(i, h) == "V":
                 nc.vector.tensor_copy(out=dst, in_=src)
             else:
                 nc.scalar.copy(out=dst, in_=src)
 
         def stage_c(i):
-            codes = work.tile([P, UNIT], U32, tag="xq", align_bytes=64, name="xq%d" % i)
-            scales = work.tile([P, UNIT], U8, tag="xs", align_bytes=64, name="xs%d" % i)
+            codes = work.tile([P, CHUNKS[i]], U32, tag="xq", align_bytes=64, name="xq%d" % i)
+            scales = work.tile([P, CHUNKS[i]], U8, tag="xs", align_bytes=64, name="xs%d" % i)
             nc.vector.quantize_mx(out=codes[:].bitcast(FP8X4), scales=scales[:], in_=grp[i][:])
             xq[i] = (codes, scales)
 
         def stage_d(i):
             codes, scales = xq[i]
-            for h in range(2):
-                a = psum.tile([P, UNIT], F32, tag="acc", bufs=3, name="acc%d_%d" % (i, h))
+            n = CHUNKS[i]
+            for m in range(2):
+                if m == 0 or n > HALF:
+                    bank = psum.tile([P, 512], F32, tag="acc", bufs=2, name="acc%d_%d" % (i, m))
+                a = bank[:, 0:n] if n > HALF else bank[:, m * HALF : m * HALF + n]
                 nc.tensor.matmul_mx(
-                    out=a[:],
-                    lhsT=w_codes[:, h * P : (h + 1) * P].bitcast(FP8X4),
-                    lhsT_scale=w_scales[:, h * P : (h + 1) * P],
+                    out=a,
+                    lhsT=w_codes[:, m * P : (m + 1) * P].bitcast(FP8X4),
+                    lhsT_scale=w_scales[:, m * P : (m + 1) * P],
                     rhs=codes[:].bitcast(FP8X4),
                     rhs_scale=scales[:],
                     start=True,
                     stop=True,
                 )
-                acc[(i, h)] = a
+                acc[(i, m)] = a
 
-        def stage_e(i):
-            for h in range(2):
-                g = gpool.tile([P, UNIT], F32, tag="g", name="g%d_%d" % (i, h))
-                nc.scalar.activation(
-                    out=g[:],
-                    in_=acc[(i, h)][:],
-                    func=ACT.Gelu_apprx_tanh,
-                    bias=bn_b[:, h : h + 1],
-                    scale=bn_s[:, h : h + 1],
-                )
-                gel[(i, h)] = g
+        def stage_e(i, m):
+            g = gpool.tile([P, CHUNKS[i]], F32, tag="g", name="g%d_%d" % (i, m))
+            nc.scalar.activation(
+                out=g[:],
+                in_=acc[(i, m)],
+                func=ACT.Gelu_apprx_tanh,
+                bias=bn_b[:, m : m + 1],
+                scale=bn_s[:, m : m + 1],
+            )
+            gel[(i, m)] = g
 
-        def stage_f(i):
-            for hb in range(2):
-                t = psum.tile([P, 2, N], F32, tag="ot", bufs=2, name="ot%d_%d" % (i, hb))
-                for jj in range(2):
-                    for h in range(2):
-                        col = (2 * hb + jj) * P
-                        nc.tensor.transpose(
-                            t[:, jj, h * P : (h + 1) * P], gel[(i, h)][:, col : col + P], ident[:]
-                        )
-                ot[(i, hb)] = t
+        def stage_f(i, h):
+            t = psum.tile([P, groups(i), N], F32, tag="ot", bufs=3, name="ot%d_%d" % (i, h))
+            for jj in range(groups(i)):
+                for m in range(2):
+                    col = (2 * h + jj) * P
+                    nc.tensor.transpose(
+                        t[:, jj, m * P : (m + 1) * P], gel[(i, m)][:, col : col + P], ident[:]
+                    )
+            ot[(i, h)] = t
 
-        def stage_g(i, hb, eng):
-            if i == NU - 1:
-                o_sb[(i, hb)] = opool.tile([P, 2 * N], F32, name="o%d_%d" % (i, hb))
-                dst = o_sb[(i, hb)][:]
-            else:
-                if hb == 0:
-                    o_sb[i] = opool.tile([P, J * N], F32, name="o%d" % i)
-                dst = o_sb[i][:, hb * 2 * N : (hb + 1) * 2 * N]
-            src = ot[(i, hb)][:].rearrange("p j n -> p (j n)")
-            if eng == "V":
+        def relu_copy(engine, dst, src):
+            if engine == "V":
                 nc.vector.tensor_scalar(
                     out=dst, in0=src, scalar1=0.0, scalar2=0.0, op0=ALU.max, op1=ALU.add
                 )
             else:
                 nc.scalar.activation(out=dst, in_=src, func=ACT.Relu)
 
-        def stage_h(i):
-            rows = out[i * UNIT : (i + 1) * UNIT, :].rearrange("(p j) n -> p j n", j=J)
-            if i == NU - 1:
-                for hb in range(2):
-                    nc.sync.dma_start(
-                        out=rows[:, 2 * hb : 2 * hb + 2, :],
-                        in_=o_sb[(i, hb)][:].rearrange("p (j n) -> p j n", j=2),
-                    )
+        def stage_g(i, h):
+            if i not in o_sb:
+                o_sb[i] = opool.tile([P, CHUNKS[i] // P, N], F32, name="o%d" % i)
+            src = ot[(i, h)]
+            if i == NC - 1:
+                for m, engine in enumerate("VS"):
+                    cols = slice(m * P, (m + 1) * P)
+                    relu_copy(engine, o_sb[i][:, 2 * h : 2 * h + groups(i), cols], src[:, :, cols])
             else:
-                nc.sync.dma_start(out=rows, in_=o_sb[i][:].rearrange("p (j n) -> p j n", j=J))
+                relu_copy(out_engine(i, h), o_sb[i][:, 2 * h : 2 * h + groups(i), :], src[:])
 
-        def b_engine(i, hb):
-            return "S" if (i < 3 and hb == 1) else "V"
-
-        def g_engine(i, hb):
-            if i == NU - 1:
-                return "V" if hb == 0 else "S"
-            if i >= NU - 3:
-                return "V"
-            if hb == 1:
-                return "S"
-            return "V" if i % 4 == 0 else "S"
+        def stage_h(i):
+            nc.sync.dma_start(
+                out=out[starts[i] : starts[i] + CHUNKS[i], :].rearrange(
+                    "(p j) n -> p j n", j=CHUNKS[i] // P
+                ),
+                in_=o_sb[i][:],
+            )
 
         def live(i):
-            return 0 <= i < NU
+            return 0 <= i < NC
 
-        for p in range(-LA, NU + LG + 1):
-            if live(p + 1):
-                stage_c(p + 1)
+        def has(i, h):
+            return live(i) and h in halves(i)
+
+        for p in range(-LA, NC + 2):
+            new = p + LA
+            old = p - 1
+            if has(new, 0):
+                stage_a(new, 0)
             if live(p):
                 stage_d(p)
-            if live(p + LA):
-                stage_a(p + LA)
-            if live(p - 1):
-                stage_f(p - 1)
-            if live(p - LG):
-                stage_g(p - LG, 0, g_engine(p - LG, 0))
-                stage_g(p - LG, 1, g_engine(p - LG, 1))
-                stage_h(p - LG)
+            if has(old, 0):
+                stage_f(old, 0)
+            if has(new, 1):
+                stage_a(new, 1)
+            if has(old, 1):
+                stage_f(old, 1)
             if live(p):
-                stage_e(p)
-            if live(p + LA):
-                stage_b(p + LA, 0, b_engine(p + LA, 0))
-                stage_b(p + LA, 1, b_engine(p + LA, 1))
+                stage_e(p, 0)
+                stage_e(p, 1)
+            for h in range(2):
+                if has(old, h) and (out_engine(old, h) == "S" or old == NC - 1):
+                    stage_g(old, h)
+            for h in range(2):
+                if has(new, h) and in_engine(new, h) == "S":
+                    stage_b(new, h)
+            for h in range(2):
+                if has(new + 1, h) and is_split(new + 1, h):
+                    stage_z(new + 1, h)
+            if live(new - 1):
+                stage_c(new - 1)
+            if has(new, 0) and in_engine(new, 0) == "V":
+                stage_b(new, 0)
+            if has(new, 1) and in_engine(new, 1) == "V":
+                stage_b(new, 1)
+            for h in range(2):
+                if has(old, h) and out_engine(old, h) == "V" and old < NC - 1:
+                    stage_g(old, h)
+            if live(old):
+                stage_h(old)
             if p == -LA:
-                prep_bn_1()
-                prep_weight()
-                prep_bn_2()
+                nc.vector.tensor_copy(out=prm_f[0:8, :], in_=prm_rows[:])
+                nc.tensor.transpose(p_t[:], prm_f[:], ident[:])
+                nc.vector.tensor_copy(out=w_grp[:], in_=w_raw[:].rearrange("p t n -> p n t"))
+                nc.vector.tensor_copy(out=prm[:], in_=p_t[:, 0:8])
+                nc.vector.tensor_scalar_add(out=veps[:], in0=prm[:, 6:8], scalar1=EPS)
+                nc.gpsimd.tensor_tensor(out=rstd[:], in0=veps[:], in1=mhalf[:], op=ALU.pow)
+                nc.vector.quantize_mx(
+                    out=w_codes[:].bitcast(FP8X4),
+                    scales=w_scales[:],
+                    in_=w_grp[:].rearrange("p n t -> p (n t)"),
+                )
             if p == -LA + 1:
-                prep_bn_3()
+                nc.vector.tensor_mul(out=bn_s[:], in0=prm[:, 0:2], in1=rstd[:])
+                nc.vector.tensor_mul(out=ms[:], in0=prm[:, 4:6], in1=bn_s[:])
+                nc.vector.tensor_sub(out=bn_b[:], in0=prm[:, 2:4], in1=ms[:])

@@ -93,10 +93,10 @@ def tile_modelnew_t_kernel(tc, x, weight, bn_gamma, bn_beta, bn_mean, bn_var, ou
             return x_sb[i][:, 2 * h : 2 * h + g, :].rearrange("p j k -> p (j k)").bitcast(F32)
 
         def is_split(i, h):
-            return i >= 3 and (h == 1 or i % 2 == 0)
+            return i >= 3 and h == 1
 
         def out_engine(i, h):
-            return "V" if i >= NC - 4 or (h == 0 and i % 3 == 0) else "S"
+            return "V" if i >= NC - 4 or (h == 0 and i % 4 == 0) else "S"
 
         def in_engine(i, h):
             return "S" if i == 0 or (i <= LA + 2 and h == 1) else "V"

@@ -19,7 +19,7 @@ FLOPS = 2 * B * K * N
 HALF = 256
 CHUNKS = [256, 256] + [512] * 14 + [256, 256]
 NC = len(CHUNKS)
-LA = 2
+LA = 3
 
 
 def tile_modelnew_t_kernel(tc, x, weight, bn_gamma, bn_beta, bn_mean, bn_var, out):
@@ -67,7 +67,7 @@ def tile_modelnew_t_kernel(tc, x, weight, bn_gamma, bn_beta, bn_mean, bn_var, ou
         w_scales = const.tile([P, N], U8, align_bytes=64)
         bn_s = const.tile([P, 2], F32)
         bn_b = const.tile([P, 2], F32)
-        p_t = psum.tile([P, P], F32, tag="ot", bufs=3)
+        p_t = psum.tile([P, P], F32, tag="ot", bufs=2)
         prm = const.tile([P, 8], F32)
         veps = const.tile([P, 2], F32)
         rstd = const.tile([P, 2], F32)
@@ -93,10 +93,10 @@ def tile_modelnew_t_kernel(tc, x, weight, bn_gamma, bn_beta, bn_mean, bn_var, ou
             return x_sb[i][:, 2 * h : 2 * h + g, :].rearrange("p j k -> p (j k)").bitcast(F32)
 
         def is_split(i, h):
-            return i >= 3 and h == 1
+            return i >= 3 and (h == 1 or i % 4 == 0)
 
         def out_engine(i, h):
-            return "V" if i >= NC - 4 or (h == 0 and i % 4 == 0) else "S"
+            return "V" if i >= NC - 4 or (h == 1 and i >= 5 and i % 4 == 0) else "S"
 
         def in_engine(i, h):
             return "S" if i == 0 or (i <= LA + 2 and h == 1) else "V"
@@ -111,7 +111,7 @@ def tile_modelnew_t_kernel(tc, x, weight, bn_gamma, bn_beta, bn_mean, bn_var, ou
 
         def stage_a(i, h):
             g = groups(i)
-            t = psum.tile([P, g, 2, P], F32, tag="xt", bufs=3, name="xt%d_%d" % (i, h))
+            t = psum.tile([P, g, 2, P], F32, tag="xt", bufs=4, name="xt%d_%d" % (i, h))
             for jj in range(g):
                 for u in range(2):
                     if is_split(i, h):
@@ -174,7 +174,7 @@ def tile_modelnew_t_kernel(tc, x, weight, bn_gamma, bn_beta, bn_mean, bn_var, ou
             gel[(i, m)] = g
 
         def stage_f(i, h):
-            t = psum.tile([P, groups(i), N], F32, tag="ot", bufs=3, name="ot%d_%d" % (i, h))
+            t = psum.tile([P, groups(i), N], F32, tag="ot", bufs=2, name="ot%d_%d" % (i, h))
             for jj in range(groups(i)):
                 for m in range(2):
                     col = (2 * h + jj) * P
@@ -219,16 +219,16 @@ def tile_modelnew_t_kernel(tc, x, weight, bn_gamma, bn_beta, bn_mean, bn_var, ou
         for p in range(-LA, NC + 2):
             new = p + LA
             old = p - 1
-            if has(new, 0):
-                stage_a(new, 0)
             if live(p):
                 stage_d(p)
             if has(old, 0):
                 stage_f(old, 0)
-            if has(new, 1):
-                stage_a(new, 1)
+            if has(new, 0):
+                stage_a(new, 0)
             if has(old, 1):
                 stage_f(old, 1)
+            if has(new, 1):
+                stage_a(new, 1)
             if live(p):
                 stage_e(p, 0)
                 stage_e(p, 1)
@@ -239,6 +239,9 @@ def tile_modelnew_t_kernel(tc, x, weight, bn_gamma, bn_beta, bn_mean, bn_var, ou
                 if has(new, h) and in_engine(new, h) == "S":
                     stage_b(new, h)
             for h in range(2):
+                if has(old, h) and out_engine(old, h) == "V" and old < NC - 1:
+                    stage_g(old, h)
+            for h in range(2):
                 if has(new + 1, h) and is_split(new + 1, h):
                     stage_z(new + 1, h)
             if live(new - 1):
@@ -247,9 +250,6 @@ def tile_modelnew_t_kernel(tc, x, weight, bn_gamma, bn_beta, bn_mean, bn_var, ou
                 stage_b(new, 0)
             if has(new, 1) and in_engine(new, 1) == "V":
                 stage_b(new, 1)
-            for h in range(2):
-                if has(old, h) and out_engine(old, h) == "V" and old < NC - 1:
-                    stage_g(old, h)
             if live(old):
                 stage_h(old)
             if p == -LA:

@@ -19,6 +19,7 @@ FLOPS = 2 * B * K * N
 HALF = 256
 CHUNKS = [256, 256] + [512] * 14 + [256, 256]
 NC = len(CHUNKS)
+SHARED = [[i] for i in range(5)] + [[i, i + 1] for i in range(5, NC - 3, 2)] + [[NC - 3], [NC - 2], [NC - 1]]
 LA = 3
 
 
@@ -37,13 +38,15 @@ def tile_modelnew_t_kernel(tc, x, weight, bn_gamma, bn_beta, bn_mean, bn_var, ou
         starts = [sum(CHUNKS[:i]) for i in range(NC)]
         x_sb = {}
         w_raw = const.tile([P, 4, N], BF16)
-        for i in range(NC):
-            rows = x[starts[i] : starts[i] + CHUNKS[i], :].rearrange(
-                "(p j) k -> p j k", j=CHUNKS[i] // P
-            )
-            t = xin.tile([P, CHUNKS[i] // P, K], BF16, name="x%d" % i)
+        for members in SHARED:
+            i = members[0]
+            total = sum(CHUNKS[m] for m in members)
+            rows = x[starts[i] : starts[i] + total, :].rearrange("(p j) k -> p j k", j=total // P)
+            t = xin.tile([P, total // P, K], BF16, name="x%d" % i)
             nc.sync.dma_start(out=t[:], in_=rows)
-            x_sb[i] = t
+            for m in members:
+                j0 = (starts[m] - starts[i]) // P
+                x_sb[m] = t[:, j0 : j0 + CHUNKS[m] // P, :]
             if i == 0:
                 for v, vec in enumerate((bn_gamma, bn_beta, bn_mean, bn_var)):
                     nc.sync.dma_start(
@@ -81,6 +84,7 @@ def tile_modelnew_t_kernel(tc, x, weight, bn_gamma, bn_beta, bn_mean, bn_var, ou
         gel = {}
         ot = {}
         o_sb = {}
+        o_all = {}
 
         def halves(i):
             return range(max(1, CHUNKS[i] // HALF))
@@ -96,7 +100,7 @@ def tile_modelnew_t_kernel(tc, x, weight, bn_gamma, bn_beta, bn_mean, bn_var, ou
             return i >= 3 and (h == 1 or i % 4 == 0)
 
         def out_engine(i, h):
-            return "V" if i >= NC - 4 or (h == 1 and i >= 5 and i % 4 == 0) else "S"
+            return "V" if i >= NC - 4 or (h == 0 and i >= 5 and i % 4 == 0) else "S"
 
         def in_engine(i, h):
             return "S" if i == 0 or (i <= LA + 2 and h == 1) else "V"
@@ -193,7 +197,13 @@ def tile_modelnew_t_kernel(tc, x, weight, bn_gamma, bn_beta, bn_mean, bn_var, ou
 
         def stage_g(i, h):
             if i not in o_sb:
-                o_sb[i] = opool.tile([P, CHUNKS[i] // P, N], F32, name="o%d" % i)
+                members = [s for s in SHARED if i in s][0]
+                total = sum(CHUNKS[m] for m in members)
+                t = opool.tile([P, total // P, N], F32, name="o%d" % i)
+                o_all[members[-1]] = (starts[i], total, t)
+                for m in members:
+                    j0 = (starts[m] - starts[i]) // P
+                    o_sb[m] = t[:, j0 : j0 + CHUNKS[m] // P, :]
             src = ot[(i, h)]
             if i == NC - 1:
                 for m, engine in enumerate("VS"):
@@ -203,11 +213,10 @@ def tile_modelnew_t_kernel(tc, x, weight, bn_gamma, bn_beta, bn_mean, bn_var, ou
                 relu_copy(out_engine(i, h), o_sb[i][:, 2 * h : 2 * h + groups(i), :], src[:])
 
         def stage_h(i):
+            start, total, t = o_all[i]
             nc.sync.dma_start(
-                out=out[starts[i] : starts[i] + CHUNKS[i], :].rearrange(
-                    "(p j) n -> p j n", j=CHUNKS[i] // P
-                ),
-                in_=o_sb[i][:],
+                out=out[start : start + total, :].rearrange("(p j) n -> p j n", j=total // P),
+                in_=t[:],
             )
 
         def live(i):
@@ -250,7 +259,7 @@ def tile_modelnew_t_kernel(tc, x, weight, bn_gamma, bn_beta, bn_mean, bn_var, ou
                 stage_b(new, 0)
             if has(new, 1) and in_engine(new, 1) == "V":
                 stage_b(new, 1)
-            if live(old):
+            if live(old) and old in o_all:
                 stage_h(old)
             if p == -LA:
                 nc.vector.tensor_copy(out=prm_f[0:8, :], in_=prm_rows[:])

from contextlib import ExitStack

import concourse.masks as masks
import concourse.mybir as mybir

F32 = mybir.dt.float32
BF16 = mybir.dt.bfloat16
U32 = mybir.dt.uint32
U8 = mybir.dt.uint8
FP8X4 = mybir.dt.float8_e4m3fn_x4
ACT = mybir.ActivationFunctionType
ALU = mybir.AluOpType

P = 128
B, K, N = 8192, 512, 256
EPS = 1e-5
FLOPS = 2 * B * K * N

HALF = 256
CHUNKS = [256, 256] + [512] * 14 + [256, 256]
NC = len(CHUNKS)
SHARED = [[i] for i in range(5)] + [[i, i + 1] for i in range(5, NC - 3, 2)] + [[NC - 3], [NC - 2], [NC - 1]]
LA = 3


def tile_modelnew_t_kernel(tc, x, weight, bn_gamma, bn_beta, bn_mean, bn_var, out):
    nc = tc.nc
    with ExitStack() as ctx:
        const = ctx.enter_context(tc.tile_pool(name="const", bufs=1))
        xin = ctx.enter_context(tc.tile_pool(name="xin", bufs=1))
        work = ctx.enter_context(tc.tile_pool(name="work", bufs=4))
        gpool = ctx.enter_context(tc.tile_pool(name="gpool", bufs=6))
        opool = ctx.enter_context(tc.tile_pool(name="opool", bufs=1))
        psum = ctx.enter_context(tc.psum_pool(name="psum", bufs=1))
        ctx.enter_context(tc.manual_schedule())

        prm_rows = const.tile([8, P], BF16)
        starts = [sum(CHUNKS[:i]) for i in range(NC)]
        x_sb = {}
        w_raw = const.tile([P, 4, N], BF16)
        for members in SHARED:
            i = members[0]
            total = sum(CHUNKS[m] for m in members)
            rows = x[starts[i] : starts[i] + total, :].rearrange("(p j) k -> p j k", j=total // P)
            t = xin.tile([P, total // P, K], BF16, name="x%d" % i)
            nc.sync.dma_start(out=t[:], in_=rows)
            for m in members:
                j0 = (starts[m] - starts[i]) // P
                x_sb[m] = t[:, j0 : j0 + CHUNKS[m] // P, :]
            if i == 0:
                for v, vec in enumerate((bn_gamma, bn_beta, bn_mean, bn_var)):
                    nc.sync.dma_start(
                        out=prm_rows[2 * v : 2 * v + 2, :], in_=vec.rearrange("(h n) -> h n", h=2)
                    )
                nc.sync.dma_start(out=w_raw[:], in_=weight.rearrange("(p t) n -> p t n", t=4))

        warm = const.tile([P, 1], F32)
        nc.vector.memset(warm[:], 0.0)
        warm2 = const.tile([P, 1], F32)
        nc.scalar.activation(out=warm2[:], in_=warm[:], func=ACT.Gelu_apprx_tanh)
        ident = const.tile([P, P], F32)
        masks.make_identity(nc, ident[:])
        prm_f = const.tile([P, P], F32)
        nc.vector.memset(prm_f[:], 0.0)
        mhalf = const.tile([P, 2], F32)
        nc.vector.memset(mhalf[:], -0.5)

        w_grp = const.tile([P, N, 4], BF16, align_bytes=64)
        w_codes = const.tile([P, N], U32, align_bytes=64)
        w_scales = const.tile([P, N], U8, align_bytes=64)
        bn_s = const.tile([P, 2], F32)
        bn_b = const.tile([P, 2], F32)
        p_t = psum.tile([P, P], F32, tag="ot", bufs=2)
        prm = const.tile([P, 8], F32)
        veps = const.tile([P, 2], F32)
        rstd = const.tile([P, 2], F32)
        ms = const.tile([P, 2], F32)

        split = {}
        xt = {}
        grp = {}
        xq = {}
        acc = {}
        gel = {}
        ot = {}
        o_sb = {}
        o_all = {}

        def halves(i):
            return range(max(1, CHUNKS[i] // HALF))

        def groups(i):
            return min(2, CHUNKS[i] // P)

        def words(i, h):
            g = groups(i)
            return x_sb[i][:, 2 * h : 2 * h + g, :].rearrange("p j k -> p (j k)").bitcast(F32)

        def is_split(i, h):
            return i >= 3 and (h == 1 or i % 4 == 0)

        def out_engine(i, h):
            return "V" if i >= NC - 4 or (h == 0 and i >= 5 and i % 4 == 0) else "S"

        def in_engine(i, h):
            return "S" if i == 0 or (i <= LA + 2 and h == 1) else "V"

        def stage_z(i, h):
            g = groups(i)
            t = work.tile([P, g, 2, P], F32, tag="z", name="z%d_%d" % (i, h))
            nc.vector.tensor_copy(
                out=t[:], in_=words(i, h).rearrange("p (j w u) -> p j u w", j=g, u=2)
            )
            split[(i, h)] = t

        def stage_a(i, h):
            g = groups(i)
            t = psum.tile([P, g, 2, P], F32, tag="xt", bufs=4, name="xt%d_%d" % (i, h))
            for jj in range(g):
                for u in range(2):
                    if is_split(i, h):
                        src = split[(i, h)][:, jj, u, :]
                    else:
                        src = words(i, h)[:, jj * (K // 2) + u : (jj + 1) * (K // 2) : 2]
                    nc.tensor.transpose(t[:, jj, u, :], src, ident[:])
            xt[(i, h)] = t

        def stage_b(i, h):
            if i not in grp:
                grp[i] = work.tile(
                    [P, 4 * CHUNKS[i]], BF16, tag="grp", align_bytes=64, name="grp%d" % i
                )
            g = groups(i)
            dst = (
                grp[i][:]
                .bitcast(F32)[:, h * 2 * HALF : h * 2 * HALF + g * 2 * P]
                .rearrange("p (j r u) -> p j r u", j=g, u=2)
            )
            src = xt[(i, h)][:].rearrange("p j u r -> p j r u")
            if in_engine(i, h) == "V":
                nc.vector.tensor_copy(out=dst, in_=src)
            else:
                nc.scalar.copy(out=dst, in_=src)

        def stage_c(i):
            codes = work.tile([P, CHUNKS[i]], U32, tag="xq", align_bytes=64, name="xq%d" % i)
            scales = work.tile([P, CHUNKS[i]], U8, tag="xs", align_bytes=64, name="xs%d" % i)
            nc.vector.quantize_mx(out=codes[:].bitcast(FP8X4), scales=scales[:], in_=grp[i][:])
            xq[i] = (codes, scales)

        def stage_d(i):
            codes, scales = xq[i]
            n = CHUNKS[i]
            for m in range(2):
                if m == 0 or n > HALF:
                    bank = psum.tile([P, 512], F32, tag="acc", bufs=2, name="acc%d_%d" % (i, m))
                a = bank[:, 0:n] if n > HALF else bank[:, m * HALF : m * HALF + n]
                nc.tensor.matmul_mx(
                    out=a,
                    lhsT=w_codes[:, m * P : (m + 1) * P].bitcast(FP8X4),
                    lhsT_scale=w_scales[:, m * P : (m + 1) * P],
                    rhs=codes[:].bitcast(FP8X4),
                    rhs_scale=scales[:],
                    start=True,
                    stop=True,
                )
                acc[(i, m)] = a

        def stage_e(i, m):
            g = gpool.tile([P, CHUNKS[i]], F32, tag="g", name="g%d_%d" % (i, m))
            nc.scalar.activation(
                out=g[:],
                in_=acc[(i, m)],
                func=ACT.Gelu_apprx_tanh,
                bias=bn_b[:, m : m + 1],
                scale=bn_s[:, m : m + 1],
            )
            gel[(i, m)] = g

        def stage_f(i, h):
            t = psum.tile([P, groups(i), N], F32, tag="ot", bufs=2, name="ot%d_%d" % (i, h))
            for jj in range(groups(i)):
                for m in range(2):
                    col = (2 * h + jj) * P
                    nc.tensor.transpose(
                        t[:, jj, m * P : (m + 1) * P], gel[(i, m)][:, col : col + P], ident[:]
                    )
            ot[(i, h)] = t

        def relu_copy(engine, dst, src):
            if engine == "V":
                nc.vector.tensor_scalar(
                    out=dst, in0=src, scalar1=0.0, scalar2=0.0, op0=ALU.max, op1=ALU.add
                )
            else:
                nc.scalar.activation(out=dst, in_=src, func=ACT.Relu)

        def stage_g(i, h):
            if i not in o_sb:
                members = [s for s in SHARED if i in s][0]
                total = sum(CHUNKS[m] for m in members)
                t = opool.tile([P, total // P, N], F32, name="o%d" % i)
                o_all[members[-1]] = (starts[i], total, t)
                for m in members:
                    j0 = (starts[m] - starts[i]) // P
                    o_sb[m] = t[:, j0 : j0 + CHUNKS[m] // P, :]
            src = ot[(i, h)]
            if i == NC - 1:
                for m, engine in enumerate("VS"):
                    cols = slice(m * P, (m + 1) * P)
                    relu_copy(engine, o_sb[i][:, 2 * h : 2 * h + groups(i), cols], src[:, :, cols])
            else:
                relu_copy(out_engine(i, h), o_sb[i][:, 2 * h : 2 * h + groups(i), :], src[:])

        def stage_h(i):
            start, total, t = o_all[i]
            nc.sync.dma_start(
                out=out[start : start + total, :].rearrange("(p j) n -> p j n", j=total // P),
                in_=t[:],
            )

        def live(i):
            return 0 <= i < NC

        def has(i, h):
            return live(i) and h in halves(i)

        for p in range(-LA, NC + 2):
            new = p + LA
            old = p - 1
            if live(p):
                stage_d(p)
            if has(old, 0):
                stage_f(old, 0)
            if has(new, 0):
                stage_a(new, 0)
            if has(old, 1):
                stage_f(old, 1)
            if has(new, 1):
                stage_a(new, 1)
            if live(p):
                stage_e(p, 0)
                stage_e(p, 1)
            for h in range(2):
                if has(old, h) and (out_engine(old, h) == "S" or old == NC - 1):
                    stage_g(old, h)
            for h in range(2):
                if has(new, h) and in_engine(new, h) == "S":
                    stage_b(new, h)
            for h in range(2):
                if has(old, h) and out_engine(old, h) == "V" and old < NC - 1:
                    stage_g(old, h)
            for h in range(2):
                if has(new + 1, h) and is_split(new + 1, h):
                    stage_z(new + 1, h)
            if live(new - 1):
                stage_c(new - 1)
            if has(new, 0) and in_engine(new, 0) == "V":
                stage_b(new, 0)
            if has(new, 1) and in_engine(new, 1) == "V":
                stage_b(new, 1)
            if live(old) and old in o_all:
                stage_h(old)
            if p == -LA:
                nc.vector.tensor_copy(out=prm_f[0:8, :], in_=prm_rows[:])
                nc.tensor.transpose(p_t[:], prm_f[:], ident[:])
                nc.vector.tensor_copy(out=w_grp[:], in_=w_raw[:].rearrange("p t n -> p n t"))
                nc.vector.tensor_copy(out=prm[:], in_=p_t[:, 0:8])
                nc.vector.tensor_scalar_add(out=veps[:], in0=prm[:, 6:8], scalar1=EPS)
                nc.gpsimd.tensor_tensor(out=rstd[:], in0=veps[:], in1=mhalf[:], op=ALU.pow)
                nc.vector.quantize_mx(
                    out=w_codes[:].bitcast(FP8X4),
                    scales=w_scales[:],
                    in_=w_grp[:].rearrange("p n t -> p (n t)"),
                )
            if p == -LA + 1:
                nc.vector.tensor_mul(out=bn_s[:], in0=prm[:, 0:2], in1=rstd[:])
                nc.vector.tensor_mul(out=ms[:], in0=prm[:, 4:6], in1=bn_s[:])
                nc.vector.tensor_sub(out=bn_b[:], in0=prm[:, 2:4], in1=ms[:])
